import numpy as np
import ml_dtypes


def mxq(x, axis, fmt="e4m3"):
    dtype, down = {"e4m3": (ml_dtypes.float8_e4m3fn, 7), "e5m2": (ml_dtypes.float8_e5m2, 14)}[fmt]
    v = np.moveaxis(np.asarray(x, np.float32).astype(ml_dtypes.bfloat16).astype(np.float64), axis, -1)
    blocks = v.reshape(v.shape[:-1] + (-1, 32))
    amax = np.abs(blocks).max(-1, keepdims=True)
    byte = np.maximum(np.where(amax > 0, np.frexp(amax)[1] - 1 + 127, 0) - down, 1)
    scale = np.exp2(byte - 127.0)
    codes = (blocks / scale).astype(np.float32).astype(dtype).astype(np.float64)
    return np.moveaxis((codes * scale).reshape(v.shape), -1, axis)


WIDE = False


def mx_kscale(k):
    if not WIDE:
        return np.ones(k)
    levels = np.array([10, -10, 5, -5, 0])
    if k % 512:
        return np.exp2(np.random.permutation(np.resize(levels, k // 32))).repeat(32)
    a = np.empty((k // 512, 16))
    for p in range(k // 512):
        a[p, :8] = np.random.permutation(np.resize(levels, 8))
        for g in range(8):
            far = levels[np.abs(levels - a[p, g]) >= 10]
            a[p, g + 8] = far[np.random.randint(len(far))]
    return np.exp2(a.ravel()).repeat(32)


BF16 = ml_dtypes.bfloat16


def bf(x):
    return np.asarray(x, np.float32).astype(BF16)


def f64(x):
    return np.asarray(x).astype(np.float64)


B, S, NH, HD = 4, 512, 12, 128
H = NH * HD


def split_heads(x):
    return x.reshape(B, S, NH, HD).transpose(0, 2, 1, 3)


def setup_inputs():
    t = mx_kscale(S)
    t = t / t.max()
    kind = np.random.randint(0, 4, (B, S))
    base = np.where(kind < 2, 0.0, np.where(kind == 2, -10000.0, np.random.standard_normal((B, S))))
    return {"model_hidden_states": bf(np.random.standard_normal((B, S, H))),
            "k_hidden_states": bf(np.random.standard_normal((B, S, H))),
            "k_embeddings": bf(np.random.standard_normal((B, S, H)) * 0.15 * np.sqrt(S) / t[None, :, None]),
            "attention_mask": bf(base + np.log(t)[None, :])}


def reference(model_hidden_states, k_hidden_states, k_embeddings, attention_mask):
    q = split_heads(f64(model_hidden_states))
    k = split_heads(f64(k_hidden_states))
    v = split_heads(f64(k_embeddings))
    energy = q @ k.transpose(0, 1, 3, 2) / np.sqrt(HD)
    m = f64(attention_mask)[:, None, None, :]
    energy = np.where(m == 0, energy, m)
    e = np.exp(energy - energy.max(-1, keepdims=True))
    attn = (mxq(e, 3, "e4m3") @ mxq(v, 2, "e4m3")) / e.sum(-1, keepdims=True)
    return attn.transpose(0, 2, 1, 3).reshape(B, S, H)

@@ -1,0 +1,288 @@
+import math
+from contextlib import ExitStack
+
+import concourse.mybir as mybir
+from concourse.masks import make_identity
+
+B, S, NH, HD = 4, 512, 12, 128
+FLOPS = 2 * 2 * B * NH * S * S * HD
+
+BF16 = mybir.dt.bfloat16
+F32 = mybir.dt.float32
+U32 = mybir.dt.uint32
+U8 = mybir.dt.uint8
+FP8X4 = mybir.dt.float8_e4m3fn_x4
+ALU = mybir.AluOpType
+ACTF = mybir.ActivationFunctionType
+
+P = 128
+NT = S // P
+GH = 4
+NG = NH // GH
+GC = GH * HD
+HEADS = B * NH
+
+
+def tile_knnattention_kernel(tc, model_hidden_states, k_hidden_states, k_embeddings, attention_mask, out):
+    nc = tc.nc
+    scale = 1.0 / math.sqrt(HD)
+    q_dram = model_hidden_states.rearrange("b (p t) c -> b p t c", t=NT)
+    k_dram = k_hidden_states.rearrange("b (a i u) c -> b a i u c", a=2, u=2)
+    v_dram = k_embeddings.rearrange("b (p t) c -> b p t c", t=NT)
+    o_dram = out.rearrange("b (p t) c -> b p t c", t=NT)
+    with ExitStack() as ctx:
+        const = ctx.enter_context(tc.tile_pool(name="const", bufs=1))
+        loads = ctx.enter_context(tc.tile_pool(name="loads", bufs=3))
+        work = ctx.enter_context(tc.tile_pool(name="work", bufs=3))
+        small = ctx.enter_context(tc.tile_pool(name="small", bufs=6))
+        psum = ctx.enter_context(tc.psum_pool(name="psum", bufs=1))
+        ctx.enter_context(tc.manual_schedule())
+
+        groups = {}
+        batch = {}
+        heads = {}
+
+        def load_mask(b):
+            mask_bf = const.tile([P, S], BF16, name="mask%d" % b)
+            nc.sync.dma_start(out=mask_bf[:], in_=attention_mask[b, :].partition_broadcast(P))
+            batch[b] = {"mask": mask_bf}
+
+        def load_group(m):
+            b, g = divmod(m, NG)
+            cols = slice(g * GC, (g + 1) * GC)
+            q_sb = loads.tile([P, NT, GC], BF16, tag="q")
+            nc.sync.dma_start(out=q_sb[:], in_=q_dram[b, :, :, cols])
+            k_sb = loads.tile([P, NT, GC], BF16, tag="k")
+            for a in range(2):
+                nc.sync.dma_start(out=k_sb[:, a:NT:2, :], in_=k_dram[b, a, :, :, cols])
+            v_sb = loads.tile([P, NT, GC], BF16, tag="v")
+            nc.sync.dma_start(out=v_sb[:], in_=v_dram[b, :, :, cols])
+            groups[m] = {"q": q_sb, "k": k_sb, "v": v_sb}
+
+        def setup_keep(b):
+            mask_k = batch[b]["mask"][:].rearrange("x (a i u) -> x u a i", a=2, u=2)
+            keep = const.tile([P, NT, P], BF16, name="keep%d" % b)
+            nc.vector.tensor_scalar(out=keep[:].rearrange("x (u a) i -> x u a i", u=2), in0=mask_k, scalar1=0.0, scalar2=None, op0=ALU.is_equal)
+            diagk = const.tile([P, NT, P], BF16, name="diagk%d" % b)
+            nc.vector.tensor_tensor(out=diagk[:], in0=keep[:],
+                                    in1=ident_bf[:].unsqueeze(1).to_broadcast([P, NT, P]), op=ALU.mult)
+            batch[b]["diagk"] = diagk
+
+        def setup_maskc(b):
+            mask_k = batch[b]["mask"][:].rearrange("x (a i u) -> x u a i", a=2, u=2)
+            maskc = const.tile([P, NT, P], F32, name="maskc%d" % b)
+            nc.vector.tensor_scalar(out=maskc[:].rearrange("x (u a) i -> x u a i", u=2), in0=mask_k, scalar1=math.sqrt(HD), scalar2=None, op0=ALU.mult)
+            batch[b]["maskc"] = maskc
+
+        def setup_mb_pe(b):
+            mb_ps = psum.tile([P, NT, P], F32, tag="qk", bufs=1)
+            for j in range(NT):
+                nc.tensor.transpose(mb_ps[:, j, :], batch[b]["maskc"][:, j, :], ident_f[:])
+            batch[b]["mb_ps"] = mb_ps
+
+        def setup_mb_copy(b):
+            mb = const.tile([P, NT, P], F32, name="mb%d" % b)
+            nc.vector.tensor_copy(out=mb[:], in_=batch[b]["mb_ps"][:])
+            batch[b]["mb"] = mb
+
+        def where(i):
+            m, hh = divmod(i, GH)
+            return m, m // NG, hh
+
+        def pe_qk_transposes(i, part):
+            m, b, hh = where(i)
+            grp = groups[m]
+            hc = slice(hh * HD, (hh + 1) * HD)
+            if part == 0:
+                qk_ps = psum.tile([P, 2 * S], BF16, tag="qk", bufs=1)
+                heads[i] = {"qk_ps": qk_ps}
+            qk_ps = heads[i]["qk_ps"]
+            for x in (2 * part, 2 * part + 1):
+                if x < NT:
+                    nc.tensor.transpose(qk_ps[:, x * P:(x + 1) * P], grp["q"][:, x, hc], ident_bf[:])
+                else:
+                    nc.tensor.transpose(qk_ps[:, x * P:(x + 1) * P], grp["k"][:, x - NT, hc],
+                                        batch[b]["diagk"][:, x - NT, :])
+
+        def act_qk_copy(i):
+            qkt = work.tile([P, 2 * S], BF16, tag="qkt", bufs=3)
+            nc.scalar.copy(out=qkt[:], in_=heads[i]["qk_ps"][:])
+            heads[i]["qkt"] = qkt
+
+        def pe_deposit(i):
+            m, b, hh = where(i)
+            mb = batch[b]["mb"]
+            banks = []
+            for t in range(NT):
+                s_ps = psum.tile([P, S], F32, tag="s", bufs=4)
+                for j in range(NT):
+                    nc.tensor.matmul(out=s_ps[:, j * P:(j + 1) * P], lhsT=mb[:, j, :], rhs=ident_f[:],
+                                     is_transpose=True, start=(j == 0), stop=False)
+                banks.append(s_ps)
+            heads[i]["s"] = banks
+
+        def pe_scores(i, t):
+            qkt = heads[i]["qkt"]
+            nc.tensor.matmul(out=heads[i]["s"][t][:], lhsT=qkt[:, t * P:(t + 1) * P], rhs=qkt[:, S:2 * S],
+                             start=False, stop=True)
+
+        def dve_max(i):
+            bias = small.tile([P, NT], F32, tag="bias")
+            ys = []
+            for t in range(NT):
+                y_sb = work.tile([P, S], F32, tag="y", bufs=6)
+                nc.vector.tensor_scalar(out=y_sb[:], in0=heads[i]["s"][t][:], scalar1=-scale, scalar2=None,
+                                        op0=ALU.mult, op1=ALU.min, accum_out=bias[:, t:t + 1])
+                ys.append(y_sb)
+            heads[i]["bias"] = bias
+            heads[i]["y"] = ys
+
+        def act_exp(i, t):
+            if t == 0:
+                rsum = small.tile([P, NT], F32, tag="rsum")
+                heads[i]["rsum"] = rsum
+                e_sb = work.tile([P, NT, S], BF16, tag="e", bufs=4)
+                heads[i]["e"] = e_sb
+            nc.scalar.activation(out=heads[i]["e"][:, t, :], in_=heads[i]["y"][t][:], func=ACTF.Exp,
+                                 bias=heads[i]["bias"][:, t:t + 1], scale=-1.0,
+                                 accum_out=heads[i]["rsum"][:, t:t + 1])
+
+        def pe_e_transposes(i):
+            banks = []
+            for half in range(2):
+                et_ps = psum.tile([P, 2, 2, P], F32, tag="et", bufs=2)
+                for tt in range(2):
+                    e_words = heads[i]["e"][:, 2 * half + tt, :].bitcast(F32)
+                    for u in range(2):
+                        nc.tensor.transpose(et_ps[:, tt, u, :], e_words[:, u * P:(u + 1) * P], ident_f[:])
+                banks.append(et_ps)
+            heads[i]["et"] = banks
+
+        def act_e_copy(i):
+            eg = work.tile([P, NT * P * NT], BF16, tag="eg", bufs=3, align_bytes=64)
+            eg_words = eg[:].bitcast(F32).rearrange("p (t q u) -> p t q u", t=NT, q=P, u=2)
+            for half in range(2):
+                nc.scalar.copy(out=eg_words[:, 2 * half:2 * half + 2, :, :],
+                               in_=heads[i]["et"][half][:].rearrange("p t u q -> p t q u"))
+            heads[i]["eg"] = eg
+
+        def dve_quant(i):
+            e_codes = work.tile([P, S], U32, tag="ec", bufs=3, align_bytes=64)
+            e_scales = work.tile([P, S], U8, tag="es", bufs=3, align_bytes=64)
+            nc.vector.quantize_mx(out=e_codes[:].bitcast(FP8X4), scales=e_scales[:], in_=heads[i]["eg"][:])
+            heads[i]["ec"] = e_codes
+            heads[i]["es"] = e_scales
+
+        def pool_v_regroup(m, hh):
+            hc = slice(hh * HD, (hh + 1) * HD)
+            if hh == 0:
+                vg = work.tile([P, GC, NT], BF16, tag="vg", bufs=2, align_bytes=64)
+                groups[m]["vg"] = vg
+            nc.gpsimd.tensor_scalar(out=groups[m]["vg"][:, hc, :].rearrange("p c (u e) -> p c u e", u=2),
+                                    in0=groups[m]["v"][:, :, hc].rearrange("p (e u) c -> p c u e", e=2),
+                                    scalar1=1.0, scalar2=0.0, op0=ALU.mult, op1=ALU.add)
+
+        def dve_v_quant(m):
+            v_codes = work.tile([P, GC], U32, tag="vc", bufs=3, align_bytes=64)
+            v_scales = work.tile([P, GC], U8, tag="vs", bufs=3, align_bytes=64)
+            nc.vector.quantize_mx(out=v_codes[:].bitcast(FP8X4), scales=v_scales[:],
+                                  in_=groups[m]["vg"][:].rearrange("p c j -> p (c j)"))
+            groups[m]["vc"] = v_codes
+            groups[m]["vs"] = v_scales
+
+        def pe_pv(i):
+            m, b, hh = where(i)
+            grp = groups[m]
+            hc = slice(hh * HD, (hh + 1) * HD)
+            o_ps = psum.tile([P, NT, HD], F32, tag="o", bufs=1)
+            for t in range(NT):
+                tq = slice(t * P, (t + 1) * P)
+                nc.tensor.matmul_mx(out=o_ps[:, t, :], lhsT=heads[i]["ec"][:, tq].bitcast(FP8X4),
+                                    lhsT_scale=heads[i]["es"][:, tq],
+                                    rhs=grp["vc"][:, hc].bitcast(FP8X4), rhs_scale=grp["vs"][:, hc],
+                                    start=True, stop=True)
+            heads[i]["o_ps"] = o_ps
+
+        def dve_recip(i):
+            recip = small.tile([P, NT], F32, tag="recip")
+            nc.vector.reciprocal(out=recip[:], in_=heads[i]["rsum"][:])
+            heads[i]["recip"] = recip
+
+        def dve_out(i):
+            m, b, hh = where(i)
+            grp = groups[m]
+            hc = slice(hh * HD, (hh + 1) * HD)
+            if hh == 0:
+                o_sb = work.tile([P, NT, GC], F32, tag="o_sb", bufs=2)
+                grp["o"] = o_sb
+            nc.vector.tensor_tensor(out=grp["o"][:, :, hc], in0=heads[i]["o_ps"][:],
+                                    in1=heads[i]["recip"][:].unsqueeze(2).to_broadcast([P, NT, HD]), op=ALU.mult)
+            g = m % NG
+            if m == B * NG - 1:
+                nc.sync.dma_start(out=o_dram[b, :, :, g * GC + hh * HD:g * GC + (hh + 1) * HD], in_=grp["o"][:, :, hc])
+            elif hh == GH - 1:
+                nc.sync.dma_start(out=o_dram[b, :, :, g * GC:(g + 1) * GC], in_=grp["o"][:])
+
+        load_mask(0)
+        load_group(0)
+        for b in range(1, B):
+            load_mask(b)
+        load_group(1)
+        load_group(2)
+        ident_bf = const.tile([P, P], BF16)
+        make_identity(nc, ident_bf[:])
+        ident_f = const.tile([P, P], F32)
+        make_identity(nc, ident_f[:])
+        setup_keep(0)
+        setup_maskc(0)
+        setup_mb_pe(0)
+        setup_mb_copy(0)
+        for hh in range(GH):
+            pool_v_regroup(0, hh)
+        for t in range(NT):
+            pe_qk_transposes(0, t)
+        act_qk_copy(0)
+
+        for h in range(HEADS + 3):
+            live = h < HEADS
+            if 0 <= h - 2 < HEADS:
+                pe_e_transposes(h - 2)
+            if live:
+                pe_deposit(h)
+                for t in range(NT):
+                    if h + 1 < HEADS:
+                        pe_qk_transposes(h + 1, t)
+                    pe_scores(h, t)
+            if 0 <= h - 3:
+                pe_pv(h - 3)
+            if 0 <= h - 2 < HEADS:
+                act_e_copy(h - 2)
+            if live:
+                dve_max(h)
+                act_exp(h, 0)
+            if h + 1 < HEADS:
+                act_qk_copy(h + 1)
+            for b in range(1, B):
+                if h == NH * b - 5:
+                    setup_mb_pe(b)
+            if live:
+                for t in range(1, NT):
+                    act_exp(h, t)
+            if 0 <= h - 3:
+                dve_recip(h - 3)
+            if 0 <= h - 2 < HEADS:
+                dve_quant(h - 2)
+            if 0 <= h - 3:
+                dve_out(h - 3)
+            if h % GH == 0 and h // GH < B * NG:
+                dve_v_quant(h // GH)
+            for b in range(1, B):
+                if h == NH * b - 6:
+                    setup_keep(b)
+                    setup_maskc(b)
+                if h == NH * b - 5:
+                    setup_mb_copy(b)
+            if h + GH < HEADS:
+                pool_v_regroup(h // GH + 1, h % GH)
+            if h % GH == 3 and h // GH + 3 < B * NG:
+                load_group(h // GH + 3)

@@ -42,100 +42,93 @@ def tile_knnattention_kernel(tc, model_hidden_states, k_hidden_states, k_embeddi
         batch = {}
         heads = {}
 
-        def load_mask(b):
-            mask_bf = const.tile([P, S], BF16, name="mask%d" % b)
-            nc.sync.dma_start(out=mask_bf[:], in_=attention_mask[b, :].partition_broadcast(P))
-            batch[b] = {"mask": mask_bf}
-
         def load_group(m):
             b, g = divmod(m, NG)
-            cols = slice(g * GC, (g + 1) * GC)
             q_sb = loads.tile([P, NT, GC], BF16, tag="q")
-            nc.sync.dma_start(out=q_sb[:], in_=q_dram[b, :, :, cols])
             k_sb = loads.tile([P, NT, GC], BF16, tag="k")
-            for a in range(2):
-                nc.sync.dma_start(out=k_sb[:, a:NT:2, :], in_=k_dram[b, a, :, :, cols])
             v_sb = loads.tile([P, NT, GC], BF16, tag="v")
-            nc.sync.dma_start(out=v_sb[:], in_=v_dram[b, :, :, cols])
+            parts = 2 if m == 0 else 1
+            w = GC // parts
+            for x in range(parts):
+                src = slice(g * GC + x * w, g * GC + (x + 1) * w)
+                dst = slice(x * w, (x + 1) * w)
+                nc.sync.dma_start(out=q_sb[:, :, dst], in_=q_dram[b, :, :, src])
+                for a in range(2):
+                    nc.sync.dma_start(out=k_sb[:, a:NT:2, dst], in_=k_dram[b, a, :, :, src])
+            nc.sync.dma_start(out=v_sb[:], in_=v_dram[b, :, :, g * GC:(g + 1) * GC])
             groups[m] = {"q": q_sb, "k": k_sb, "v": v_sb}
 
-        def setup_keep(b):
-            mask_k = batch[b]["mask"][:].rearrange("x (a i u) -> x u a i", a=2, u=2)
-            keep = const.tile([P, NT, P], BF16, name="keep%d" % b)
-            nc.vector.tensor_scalar(out=keep[:].rearrange("x (u a) i -> x u a i", u=2), in0=mask_k, scalar1=0.0, scalar2=None, op0=ALU.is_equal)
-            diagk = const.tile([P, NT, P], BF16, name="diagk%d" % b)
-            nc.vector.tensor_tensor(out=diagk[:], in0=keep[:],
-                                    in1=ident_bf[:].unsqueeze(1).to_broadcast([P, NT, P]), op=ALU.mult)
-            batch[b]["diagk"] = diagk
+        def setup_masks():
+            mrow = const.tile([P, S], BF16, name="mrow")
+            nc.vector.memset(mrow[:], 0.0)
+            nc.scalar.dma_start(out=mrow[0:B, :], in_=attention_mask[:, :])
+            return mrow
 
-        def setup_maskc(b):
-            mask_k = batch[b]["mask"][:].rearrange("x (a i u) -> x u a i", a=2, u=2)
-            maskc = const.tile([P, NT, P], F32, name="maskc%d" % b)
-            nc.vector.tensor_scalar(out=maskc[:].rearrange("x (u a) i -> x u a i", u=2), in0=mask_k, scalar1=math.sqrt(HD), scalar2=None, op0=ALU.mult)
-            batch[b]["maskc"] = maskc
-
-        def setup_mb_pe(b):
-            mb_ps = psum.tile([P, NT, P], F32, tag="qk", bufs=1)
+        def setup_mask_columns(mrow):
+            mt_ps = psum.tile([P, NT, P], BF16, tag="qk", bufs=1)
             for j in range(NT):
-                nc.tensor.transpose(mb_ps[:, j, :], batch[b]["maskc"][:, j, :], ident_f[:])
-            batch[b]["mb_ps"] = mb_ps
+                u, a = divmod(j, 2)
+                nc.tensor.transpose(mt_ps[:, j, :], mrow[:, 256 * a + u:256 * (a + 1):2], ident_bf[:])
+            keep = const.tile([P, NT, B], F32, name="keep")
+            nc.vector.tensor_scalar(out=keep[:], in0=mt_ps[:, :, 0:B], scalar1=0.0, scalar2=None, op0=ALU.is_equal)
+            maskc = const.tile([P, NT, B], F32, name="maskc")
+            nc.vector.tensor_scalar(out=maskc[:], in0=mt_ps[:, :, 0:B], scalar1=math.sqrt(HD), scalar2=None, op0=ALU.mult)
+            return keep, maskc
 
-        def setup_mb_copy(b):
+        def setup_batch(b, engine):
+            diagk = const.tile([P, NT, P], BF16, name="diagk%d" % b)
+            for j in range(NT):
+                engine.tensor_scalar(out=diagk[:, j, :], in0=ident_bf[:], scalar1=keep[:, j, b:b + 1], scalar2=0.0,
+                                     op0=ALU.mult, op1=ALU.add)
             mb = const.tile([P, NT, P], F32, name="mb%d" % b)
-            nc.vector.tensor_copy(out=mb[:], in_=batch[b]["mb_ps"][:])
-            batch[b]["mb"] = mb
+            engine.tensor_scalar(out=mb[:], in0=maskc[:, :, b:b + 1].to_broadcast([P, NT, P]), scalar1=1.0, scalar2=0.0,
+                                 op0=ALU.mult, op1=ALU.add)
+            batch[b] = {"diagk": diagk, "mb": mb}
 
         def where(i):
             m, hh = divmod(i, GH)
             return m, m // NG, hh
 
-        def pe_qk_transposes(i, part):
+        def pe_qk_transposes(i, half):
             m, b, hh = where(i)
             grp = groups[m]
             hc = slice(hh * HD, (hh + 1) * HD)
-            if part == 0:
+            if half == 0:
                 qk_ps = psum.tile([P, 2 * S], BF16, tag="qk", bufs=1)
                 heads[i] = {"qk_ps": qk_ps}
             qk_ps = heads[i]["qk_ps"]
-            for x in (2 * part, 2 * part + 1):
-                if x < NT:
+            for x in range(NT):
+                if half == 0:
                     nc.tensor.transpose(qk_ps[:, x * P:(x + 1) * P], grp["q"][:, x, hc], ident_bf[:])
                 else:
-                    nc.tensor.transpose(qk_ps[:, x * P:(x + 1) * P], grp["k"][:, x - NT, hc],
-                                        batch[b]["diagk"][:, x - NT, :])
+                    nc.tensor.transpose(qk_ps[:, S + x * P:S + (x + 1) * P], grp["k"][:, x, hc], batch[b]["diagk"][:, x, :])
 
         def act_qk_copy(i):
             qkt = work.tile([P, 2 * S], BF16, tag="qkt", bufs=3)
             nc.scalar.copy(out=qkt[:], in_=heads[i]["qk_ps"][:])
             heads[i]["qkt"] = qkt
 
-        def pe_deposit(i):
-            m, b, hh = where(i)
-            mb = batch[b]["mb"]
-            banks = []
-            for t in range(NT):
-                s_ps = psum.tile([P, S], F32, tag="s", bufs=4)
-                for j in range(NT):
-                    nc.tensor.matmul(out=s_ps[:, j * P:(j + 1) * P], lhsT=mb[:, j, :], rhs=ident_f[:],
-                                     is_transpose=True, start=(j == 0), stop=False)
-                banks.append(s_ps)
-            heads[i]["s"] = banks
+        def pe_deposit(i, t):
+            mb = batch[where(i)[1]]["mb"]
+            s_ps = psum.tile([P, S], F32, tag="s", bufs=4)
+            for j in range(NT):
+                nc.tensor.matmul(out=s_ps[:, j * P:(j + 1) * P], lhsT=mb[:, j, :], rhs=ident_f[:],
+                                 is_transpose=True, start=(j == 0), stop=False)
+            heads[i]["s%d" % t] = s_ps
 
         def pe_scores(i, t):
             qkt = heads[i]["qkt"]
-            nc.tensor.matmul(out=heads[i]["s"][t][:], lhsT=qkt[:, t * P:(t + 1) * P], rhs=qkt[:, S:2 * S],
+            nc.tensor.matmul(out=heads[i]["s%d" % t][:], lhsT=qkt[:, t * P:(t + 1) * P], rhs=qkt[:, S:2 * S],
                              start=False, stop=True)
 
-        def dve_max(i):
-            bias = small.tile([P, NT], F32, tag="bias")
-            ys = []
-            for t in range(NT):
-                y_sb = work.tile([P, S], F32, tag="y", bufs=6)
-                nc.vector.tensor_scalar(out=y_sb[:], in0=heads[i]["s"][t][:], scalar1=-scale, scalar2=None,
-                                        op0=ALU.mult, op1=ALU.min, accum_out=bias[:, t:t + 1])
-                ys.append(y_sb)
-            heads[i]["bias"] = bias
-            heads[i]["y"] = ys
+        def dve_max(i, t):
+            if t == 0:
+                bias = small.tile([P, NT], F32, tag="bias")
+                heads[i]["bias"] = bias
+            y_sb = work.tile([P, S], F32, tag="y", bufs=6)
+            nc.vector.tensor_scalar(out=y_sb[:], in0=heads[i]["s%d" % t][:], scalar1=-scale, scalar2=None,
+                                    op0=ALU.mult, op1=ALU.min, accum_out=heads[i]["bias"][:, t:t + 1])
+            heads[i]["y%d" % t] = y_sb
 
         def act_exp(i, t):
             if t == 0:
@@ -143,35 +136,36 @@ def tile_knnattention_kernel(tc, model_hidden_states, k_hidden_states, k_embeddi
                 heads[i]["rsum"] = rsum
                 e_sb = work.tile([P, NT, S], BF16, tag="e", bufs=4)
                 heads[i]["e"] = e_sb
-            nc.scalar.activation(out=heads[i]["e"][:, t, :], in_=heads[i]["y"][t][:], func=ACTF.Exp,
+            nc.scalar.activation(out=heads[i]["e"][:, t, :], in_=heads[i]["y%d" % t][:], func=ACTF.Exp,
                                  bias=heads[i]["bias"][:, t:t + 1], scale=-1.0,
                                  accum_out=heads[i]["rsum"][:, t:t + 1])
 
-        def pe_e_transposes(i):
-            banks = []
-            for half in range(2):
-                et_ps = psum.tile([P, 2, 2, P], F32, tag="et", bufs=2)
-                for tt in range(2):
-                    e_words = heads[i]["e"][:, 2 * half + tt, :].bitcast(F32)
-                    for u in range(2):
-                        nc.tensor.transpose(et_ps[:, tt, u, :], e_words[:, u * P:(u + 1) * P], ident_f[:])
-                banks.append(et_ps)
-            heads[i]["et"] = banks
+        def pe_e_transposes(i, half):
+            et_ps = psum.tile([P, 2, 2, P], F32, tag="et", bufs=1)
+            for tt in range(2):
+                e_words = heads[i]["e"][:, 2 * half + tt, :].bitcast(F32)
+                for u in range(2):
+                    nc.tensor.transpose(et_ps[:, tt, u, :], e_words[:, u * P:(u + 1) * P], ident_f[:])
+            heads[i]["et%d" % half] = et_ps
 
-        def act_e_copy(i):
-            eg = work.tile([P, NT * P * NT], BF16, tag="eg", bufs=3, align_bytes=64)
-            eg_words = eg[:].bitcast(F32).rearrange("p (t q u) -> p t q u", t=NT, q=P, u=2)
-            for half in range(2):
-                nc.scalar.copy(out=eg_words[:, 2 * half:2 * half + 2, :, :],
-                               in_=heads[i]["et"][half][:].rearrange("p t u q -> p t q u"))
-            heads[i]["eg"] = eg
+        def act_e_copy(i, half):
+            if half == 0:
+                eg = work.tile([P, NT * P * NT], BF16, tag="eg", bufs=3, align_bytes=64)
+                heads[i]["eg"] = eg
+            eg_words = heads[i]["eg"][:].bitcast(F32).rearrange("p (t q u) -> p t q u", t=NT, q=P, u=2)
+            nc.scalar.copy(out=eg_words[:, 2 * half:2 * half + 2, :, :],
+                           in_=heads[i]["et%d" % half][:].rearrange("p t u q -> p t q u"))
 
-        def dve_quant(i):
-            e_codes = work.tile([P, S], U32, tag="ec", bufs=3, align_bytes=64)
-            e_scales = work.tile([P, S], U8, tag="es", bufs=3, align_bytes=64)
-            nc.vector.quantize_mx(out=e_codes[:].bitcast(FP8X4), scales=e_scales[:], in_=heads[i]["eg"][:])
-            heads[i]["ec"] = e_codes
-            heads[i]["es"] = e_scales
+        def dve_quant(i, part, parts):
+            if part == 0:
+                e_codes = work.tile([P, S], U32, tag="ec", bufs=3, align_bytes=64)
+                e_scales = work.tile([P, S], U8, tag="es", bufs=3, align_bytes=64)
+                heads[i]["ec"] = e_codes
+                heads[i]["es"] = e_scales
+            w = S // parts
+            qs = slice(part * w, (part + 1) * w)
+            nc.vector.quantize_mx(out=heads[i]["ec"][:, qs].bitcast(FP8X4), scales=heads[i]["es"][:, qs],
+                                  in_=heads[i]["eg"][:, part * w * NT:(part + 1) * w * NT])
 
         def pool_v_regroup(m, hh):
             hc = slice(hh * HD, (hh + 1) * HD)
@@ -190,99 +184,102 @@ def tile_knnattention_kernel(tc, model_hidden_states, k_hidden_states, k_embeddi
             groups[m]["vc"] = v_codes
             groups[m]["vs"] = v_scales
 
-        def pe_pv(i):
+        def pe_pv(i, half):
             m, b, hh = where(i)
             grp = groups[m]
             hc = slice(hh * HD, (hh + 1) * HD)
-            o_ps = psum.tile([P, NT, HD], F32, tag="o", bufs=1)
-            for t in range(NT):
-                tq = slice(t * P, (t + 1) * P)
-                nc.tensor.matmul_mx(out=o_ps[:, t, :], lhsT=heads[i]["ec"][:, tq].bitcast(FP8X4),
+            o_ps = psum.tile([P, 2, HD], F32, tag="o", bufs=2)
+            for tt in range(2):
+                tq = slice((2 * half + tt) * P, (2 * half + tt + 1) * P)
+                nc.tensor.matmul_mx(out=o_ps[:, tt, :], lhsT=heads[i]["ec"][:, tq].bitcast(FP8X4),
                                     lhsT_scale=heads[i]["es"][:, tq],
                                     rhs=grp["vc"][:, hc].bitcast(FP8X4), rhs_scale=grp["vs"][:, hc],
                                     start=True, stop=True)
-            heads[i]["o_ps"] = o_ps
+            heads[i]["o%d" % half] = o_ps
 
         def dve_recip(i):
             recip = small.tile([P, NT], F32, tag="recip")
             nc.vector.reciprocal(out=recip[:], in_=heads[i]["rsum"][:])
             heads[i]["recip"] = recip
 
-        def dve_out(i):
+        def dve_out(i, half):
             m, b, hh = where(i)
             grp = groups[m]
             hc = slice(hh * HD, (hh + 1) * HD)
-            if hh == 0:
+            ts = slice(2 * half, 2 * half + 2)
+            if hh == 0 and half == 0:
                 o_sb = work.tile([P, NT, GC], F32, tag="o_sb", bufs=2)
                 grp["o"] = o_sb
-            nc.vector.tensor_tensor(out=grp["o"][:, :, hc], in0=heads[i]["o_ps"][:],
-                                    in1=heads[i]["recip"][:].unsqueeze(2).to_broadcast([P, NT, HD]), op=ALU.mult)
+            nc.vector.tensor_tensor(out=grp["o"][:, ts, hc], in0=heads[i]["o%d" % half][:],
+                                    in1=heads[i]["recip"][:, ts].unsqueeze(2).to_broadcast([P, 2, HD]), op=ALU.mult)
             g = m % NG
             if m == B * NG - 1:
-                nc.sync.dma_start(out=o_dram[b, :, :, g * GC + hh * HD:g * GC + (hh + 1) * HD], in_=grp["o"][:, :, hc])
-            elif hh == GH - 1:
+                nc.sync.dma_start(out=o_dram[b, :, ts, g * GC + hh * HD:g * GC + (hh + 1) * HD], in_=grp["o"][:, ts, hc])
+            elif hh == GH - 1 and half == 1:
                 nc.sync.dma_start(out=o_dram[b, :, :, g * GC:(g + 1) * GC], in_=grp["o"][:])
 
-        load_mask(0)
+        mrow = setup_masks()
         load_group(0)
-        for b in range(1, B):
-            load_mask(b)
         load_group(1)
         load_group(2)
         ident_bf = const.tile([P, P], BF16)
         make_identity(nc, ident_bf[:])
         ident_f = const.tile([P, P], F32)
         make_identity(nc, ident_f[:])
-        setup_keep(0)
-        setup_maskc(0)
-        setup_mb_pe(0)
-        setup_mb_copy(0)
+        keep, maskc = setup_mask_columns(mrow)
+        setup_batch(0, nc.vector)
         for hh in range(GH):
             pool_v_regroup(0, hh)
-        for t in range(NT):
-            pe_qk_transposes(0, t)
+        for half in range(2):
+            pe_qk_transposes(0, half)
         act_qk_copy(0)
 
+        def live(i):
+            return 0 <= i < HEADS
+
         for h in range(HEADS + 3):
-            live = h < HEADS
-            if 0 <= h - 2 < HEADS:
-                pe_e_transposes(h - 2)
-            if live:
-                pe_deposit(h)
-                for t in range(NT):
-                    if h + 1 < HEADS:
-                        pe_qk_transposes(h + 1, t)
-                    pe_scores(h, t)
-            if 0 <= h - 3:
-                pe_pv(h - 3)
-            if 0 <= h - 2 < HEADS:
-                act_e_copy(h - 2)
-            if live:
-                dve_max(h)
-                act_exp(h, 0)
-            if h + 1 < HEADS:
-                act_qk_copy(h + 1)
-            for b in range(1, B):
-                if h == NH * b - 5:
-                    setup_mb_pe(b)
-            if live:
-                for t in range(1, NT):
-                    act_exp(h, t)
-            if 0 <= h - 3:
-                dve_recip(h - 3)
-            if 0 <= h - 2 < HEADS:
-                dve_quant(h - 2)
-            if 0 <= h - 3:
-                dve_out(h - 3)
-            if h % GH == 0 and h // GH < B * NG:
+            for half in range(2):
+                t0, t1 = 2 * half, 2 * half + 1
+                if live(h - 2):
+                    pe_e_transposes(h - 2, half)
+                if live(h + 1):
+                    pe_qk_transposes(h + 1, half)
+                if live(h):
+                    pe_deposit(h, t0)
+                    pe_deposit(h, t1)
+                if live(h):
+                    pe_scores(h, t0)
+                if live(h - 3):
+                    pe_pv(h - 3, half)
+                if live(h):
+                    pe_scores(h, t1)
+                if live(h - 2):
+                    act_e_copy(h - 2, half)
+                if half == 1 and live(h + 1):
+                    act_qk_copy(h + 1)
+                if half == 0:
+                    if live(h - 1):
+                        act_exp(h - 1, 2)
+                        act_exp(h - 1, 3)
+                elif live(h):
+                    act_exp(h, 0)
+                    act_exp(h, 1)
+                if h - 2 == HEADS - 1:
+                    dve_quant(h - 2, half, 2)
+                elif half == 1 and live(h - 2):
+                    dve_quant(h - 2, 0, 1)
+                if live(h):
+                    dve_max(h, t0)
+                    dve_max(h, t1)
+                if live(h - 3):
+                    if half == 0:
+                        dve_recip(h - 3)
+                    dve_out(h - 3, half)
+            if h % GH == 1 and h // GH < B * NG:
                 dve_v_quant(h // GH)
-            for b in range(1, B):
-                if h == NH * b - 6:
-                    setup_keep(b)
-                    setup_maskc(b)
-                if h == NH * b - 5:
-                    setup_mb_copy(b)
             if h + GH < HEADS:
                 pool_v_regroup(h // GH + 1, h % GH)
+            if h % NH == 4 and h // NH + 1 < B:
+                setup_batch(h // NH + 1, nc.gpsimd)
             if h % GH == 3 and h // GH + 3 < B * NG:
                 load_group(h // GH + 3)

@@ -268,12 +268,12 @@ def tile_knnattention_kernel(tc, model_hidden_states, k_hidden_states, k_embeddi
                     dve_quant(h - 2, half, 2)
                 elif half == 1 and live(h - 2):
                     dve_quant(h - 2, 0, 1)
+                if half == 0 and live(h - 3):
+                    dve_recip(h - 3)
                 if live(h):
                     dve_max(h, t0)
                     dve_max(h, t1)
                 if live(h - 3):
-                    if half == 0:
-                        dve_recip(h - 3)
                     dve_out(h - 3, half)
             if h % GH == 1 and h // GH < B * NG:
                 dve_v_quant(h // GH)

@@ -141,20 +141,20 @@ def tile_knnattention_kernel(tc, model_hidden_states, k_hidden_states, k_embeddi
                                  accum_out=heads[i]["rsum"][:, t:t + 1])
 
         def pe_e_transposes(i, half):
-            et_ps = psum.tile([P, 2, 2, P], F32, tag="et", bufs=1)
+            late = i == HEADS - 1 or (i == HEADS - 2 and half == 1)
+            et_ps = psum.tile([P, 2, 2, P], F32, tag="s" if late else "et", bufs=4 if late else 2)
             for tt in range(2):
                 e_words = heads[i]["e"][:, 2 * half + tt, :].bitcast(F32)
                 for u in range(2):
                     nc.tensor.transpose(et_ps[:, tt, u, :], e_words[:, u * P:(u + 1) * P], ident_f[:])
             heads[i]["et%d" % half] = et_ps
 
-        def act_e_copy(i, half):
+        def e_copy(i, half, copy):
             if half == 0:
                 eg = work.tile([P, NT * P * NT], BF16, tag="eg", bufs=3, align_bytes=64)
                 heads[i]["eg"] = eg
             eg_words = heads[i]["eg"][:].bitcast(F32).rearrange("p (t q u) -> p t q u", t=NT, q=P, u=2)
-            nc.scalar.copy(out=eg_words[:, 2 * half:2 * half + 2, :, :],
-                           in_=heads[i]["et%d" % half][:].rearrange("p t u q -> p t q u"))
+            copy(out=eg_words[:, 2 * half:2 * half + 2, :, :], in_=heads[i]["et%d" % half][:].rearrange("p t u q -> p t q u"))
 
         def dve_quant(i, part, parts):
             if part == 0:
@@ -184,38 +184,37 @@ def tile_knnattention_kernel(tc, model_hidden_states, k_hidden_states, k_embeddi
             groups[m]["vc"] = v_codes
             groups[m]["vs"] = v_scales
 
-        def pe_pv(i, half):
+        def pe_pv(i):
             m, b, hh = where(i)
             grp = groups[m]
             hc = slice(hh * HD, (hh + 1) * HD)
-            o_ps = psum.tile([P, 2, HD], F32, tag="o", bufs=2)
-            for tt in range(2):
-                tq = slice((2 * half + tt) * P, (2 * half + tt + 1) * P)
-                nc.tensor.matmul_mx(out=o_ps[:, tt, :], lhsT=heads[i]["ec"][:, tq].bitcast(FP8X4),
+            o_ps = psum.tile([P, NT, HD], F32, tag="o", bufs=1)
+            for t in range(NT):
+                tq = slice(t * P, (t + 1) * P)
+                nc.tensor.matmul_mx(out=o_ps[:, t, :], lhsT=heads[i]["ec"][:, tq].bitcast(FP8X4),
                                     lhsT_scale=heads[i]["es"][:, tq],
                                     rhs=grp["vc"][:, hc].bitcast(FP8X4), rhs_scale=grp["vs"][:, hc],
                                     start=True, stop=True)
-            heads[i]["o%d" % half] = o_ps
+            heads[i]["o"] = o_ps
 
         def dve_recip(i):
             recip = small.tile([P, NT], F32, tag="recip")
             nc.vector.reciprocal(out=recip[:], in_=heads[i]["rsum"][:])
             heads[i]["recip"] = recip
 
-        def dve_out(i, half):
+        def dve_out(i):
             m, b, hh = where(i)
             grp = groups[m]
             hc = slice(hh * HD, (hh + 1) * HD)
-            ts = slice(2 * half, 2 * half + 2)
-            if hh == 0 and half == 0:
+            if hh == 0:
                 o_sb = work.tile([P, NT, GC], F32, tag="o_sb", bufs=2)
                 grp["o"] = o_sb
-            nc.vector.tensor_tensor(out=grp["o"][:, ts, hc], in0=heads[i]["o%d" % half][:],
-                                    in1=heads[i]["recip"][:, ts].unsqueeze(2).to_broadcast([P, 2, HD]), op=ALU.mult)
+            nc.vector.tensor_tensor(out=grp["o"][:, :, hc], in0=heads[i]["o"][:],
+                                    in1=heads[i]["recip"][:].unsqueeze(2).to_broadcast([P, NT, HD]), op=ALU.mult)
             g = m % NG
             if m == B * NG - 1:
-                nc.sync.dma_start(out=o_dram[b, :, ts, g * GC + hh * HD:g * GC + (hh + 1) * HD], in_=grp["o"][:, ts, hc])
-            elif hh == GH - 1 and half == 1:
+                nc.sync.dma_start(out=o_dram[b, :, :, g * GC + hh * HD:g * GC + (hh + 1) * HD], in_=grp["o"][:, :, hc])
+            elif hh == GH - 1:
                 nc.sync.dma_start(out=o_dram[b, :, :, g * GC:(g + 1) * GC], in_=grp["o"][:])
 
         mrow = setup_masks()
@@ -237,24 +236,25 @@ def tile_knnattention_kernel(tc, model_hidden_states, k_hidden_states, k_embeddi
         def live(i):
             return 0 <= i < HEADS
 
-        for h in range(HEADS + 3):
+        for h in range(HEADS):
             for half in range(2):
                 t0, t1 = 2 * half, 2 * half + 1
                 if live(h - 2):
                     pe_e_transposes(h - 2, half)
-                if live(h + 1):
+                if live(h + 1) and h > 0:
                     pe_qk_transposes(h + 1, half)
                 if live(h):
                     pe_deposit(h, t0)
                     pe_deposit(h, t1)
-                if live(h):
                     pe_scores(h, t0)
-                if live(h - 3):
-                    pe_pv(h - 3, half)
+                if half == 0 and live(h - 3):
+                    pe_pv(h - 3)
                 if live(h):
                     pe_scores(h, t1)
+                if h == 0:
+                    pe_qk_transposes(1, half)
                 if live(h - 2):
-                    act_e_copy(h - 2, half)
+                    e_copy(h - 2, half, nc.scalar.copy)
                 if half == 1 and live(h + 1):
                     act_qk_copy(h + 1)
                 if half == 0:
@@ -264,17 +264,15 @@ def tile_knnattention_kernel(tc, model_hidden_states, k_hidden_states, k_embeddi
                 elif live(h):
                     act_exp(h, 0)
                     act_exp(h, 1)
-                if h - 2 == HEADS - 1:
-                    dve_quant(h - 2, half, 2)
-                elif half == 1 and live(h - 2):
+                if half == 1 and live(h - 2):
                     dve_quant(h - 2, 0, 1)
-                if half == 0 and live(h - 3):
-                    dve_recip(h - 3)
                 if live(h):
                     dve_max(h, t0)
                     dve_max(h, t1)
-                if live(h - 3):
-                    dve_out(h - 3, half)
+                if half == 0 and live(h - 3):
+                    dve_out(h - 3)
+                if half == 0 and live(h - 2):
+                    dve_recip(h - 2)
             if h % GH == 1 and h // GH < B * NG:
                 dve_v_quant(h // GH)
             if h + GH < HEADS:
@@ -283,3 +281,25 @@ def tile_knnattention_kernel(tc, model_hidden_states, k_hidden_states, k_embeddi
                 setup_batch(h // NH + 1, nc.gpsimd)
             if h % GH == 3 and h // GH + 3 < B * NG:
                 load_group(h // GH + 3)
+
+        a, b, c = HEADS - 3, HEADS - 2, HEADS - 1
+        pe_e_transposes(b, 0)
+        pe_e_transposes(b, 1)
+        e_copy(b, 0, nc.scalar.copy)
+        act_exp(c, 2)
+        act_exp(c, 3)
+        e_copy(b, 1, nc.vector.tensor_copy)
+        dve_recip(b)
+        pe_pv(a)
+        dve_out(a)
+        for half in range(2):
+            pe_e_transposes(c, half)
+            e_copy(c, half, nc.scalar.copy)
+        dve_recip(c)
+        dve_quant(b, 0, 1)
+        dve_quant(c, 0, 2)
+        pe_pv(b)
+        dve_out(b)
+        dve_quant(c, 1, 2)
+        pe_pv(c)
+        dve_out(c)

import math
from contextlib import ExitStack

import concourse.mybir as mybir
from concourse.masks import make_identity

B, S, NH, HD = 4, 512, 12, 128
FLOPS = 2 * 2 * B * NH * S * S * HD

BF16 = mybir.dt.bfloat16
F32 = mybir.dt.float32
U32 = mybir.dt.uint32
U8 = mybir.dt.uint8
FP8X4 = mybir.dt.float8_e4m3fn_x4
ALU = mybir.AluOpType
ACTF = mybir.ActivationFunctionType

P = 128
NT = S // P
GH = 4
NG = NH // GH
GC = GH * HD
HEADS = B * NH


def tile_knnattention_kernel(tc, model_hidden_states, k_hidden_states, k_embeddings, attention_mask, out):
    nc = tc.nc
    scale = 1.0 / math.sqrt(HD)
    q_dram = model_hidden_states.rearrange("b (p t) c -> b p t c", t=NT)
    k_dram = k_hidden_states.rearrange("b (a i u) c -> b a i u c", a=2, u=2)
    v_dram = k_embeddings.rearrange("b (p t) c -> b p t c", t=NT)
    o_dram = out.rearrange("b (p t) c -> b p t c", t=NT)
    with ExitStack() as ctx:
        const = ctx.enter_context(tc.tile_pool(name="const", bufs=1))
        loads = ctx.enter_context(tc.tile_pool(name="loads", bufs=3))
        work = ctx.enter_context(tc.tile_pool(name="work", bufs=3))
        small = ctx.enter_context(tc.tile_pool(name="small", bufs=6))
        psum = ctx.enter_context(tc.psum_pool(name="psum", bufs=1))
        ctx.enter_context(tc.manual_schedule())

        groups = {}
        batch = {}
        heads = {}

        def load_group(m):
            b, g = divmod(m, NG)
            q_sb = loads.tile([P, NT, GC], BF16, tag="q")
            k_sb = loads.tile([P, NT, GC], BF16, tag="k")
            v_sb = loads.tile([P, NT, GC], BF16, tag="v")
            parts = 2 if m == 0 else 1
            w = GC // parts
            for x in range(parts):
                src = slice(g * GC + x * w, g * GC + (x + 1) * w)
                dst = slice(x * w, (x + 1) * w)
                nc.sync.dma_start(out=q_sb[:, :, dst], in_=q_dram[b, :, :, src])
                for a in range(2):
                    nc.sync.dma_start(out=k_sb[:, a:NT:2, dst], in_=k_dram[b, a, :, :, src])
            nc.sync.dma_start(out=v_sb[:], in_=v_dram[b, :, :, g * GC:(g + 1) * GC])
            groups[m] = {"q": q_sb, "k": k_sb, "v": v_sb}

        def setup_masks():
            mrow = const.tile([P, S], BF16, name="mrow")
            nc.vector.memset(mrow[:], 0.0)
            nc.scalar.dma_start(out=mrow[0:B, :], in_=attention_mask[:, :])
            return mrow

        def setup_mask_columns(mrow):
            mt_ps = psum.tile([P, NT, P], BF16, tag="qk", bufs=1)
            for j in range(NT):
                u, a = divmod(j, 2)
                nc.tensor.transpose(mt_ps[:, j, :], mrow[:, 256 * a + u:256 * (a + 1):2], ident_bf[:])
            keep = const.tile([P, NT, B], F32, name="keep")
            nc.vector.tensor_scalar(out=keep[:], in0=mt_ps[:, :, 0:B], scalar1=0.0, scalar2=None, op0=ALU.is_equal)
            maskc = const.tile([P, NT, B], F32, name="maskc")
            nc.vector.tensor_scalar(out=maskc[:], in0=mt_ps[:, :, 0:B], scalar1=math.sqrt(HD), scalar2=None, op0=ALU.mult)
            return keep, maskc

        def setup_batch(b, engine):
            diagk = const.tile([P, NT, P], BF16, name="diagk%d" % b)
            for j in range(NT):
                engine.tensor_scalar(out=diagk[:, j, :], in0=ident_bf[:], scalar1=keep[:, j, b:b + 1], scalar2=0.0,
                                     op0=ALU.mult, op1=ALU.add)
            mb = const.tile([P, NT, P], F32, name="mb%d" % b)
            engine.tensor_scalar(out=mb[:], in0=maskc[:, :, b:b + 1].to_broadcast([P, NT, P]), scalar1=1.0, scalar2=0.0,
                                 op0=ALU.mult, op1=ALU.add)
            batch[b] = {"diagk": diagk, "mb": mb}

        def where(i):
            m, hh = divmod(i, GH)
            return m, m // NG, hh

        def pe_qk_transposes(i, half):
            m, b, hh = where(i)
            grp = groups[m]
            hc = slice(hh * HD, (hh + 1) * HD)
            if half == 0:
                qk_ps = psum.tile([P, 2 * S], BF16, tag="qk", bufs=1)
                heads[i] = {"qk_ps": qk_ps}
            qk_ps = heads[i]["qk_ps"]
            for x in range(NT):
                if half == 0:
                    nc.tensor.transpose(qk_ps[:, x * P:(x + 1) * P], grp["q"][:, x, hc], ident_bf[:])
                else:
                    nc.tensor.transpose(qk_ps[:, S + x * P:S + (x + 1) * P], grp["k"][:, x, hc], batch[b]["diagk"][:, x, :])

        def act_qk_copy(i):
            qkt = work.tile([P, 2 * S], BF16, tag="qkt", bufs=3)
            nc.scalar.copy(out=qkt[:], in_=heads[i]["qk_ps"][:])
            heads[i]["qkt"] = qkt

        def pe_deposit(i, t):
            mb = batch[where(i)[1]]["mb"]
            s_ps = psum.tile([P, S], F32, tag="s", bufs=4)
            for j in range(NT):
                nc.tensor.matmul(out=s_ps[:, j * P:(j + 1) * P], lhsT=mb[:, j, :], rhs=ident_f[:],
                                 is_transpose=True, start=(j == 0), stop=False)
            heads[i]["s%d" % t] = s_ps

        def pe_scores(i, t):
            qkt = heads[i]["qkt"]
            nc.tensor.matmul(out=heads[i]["s%d" % t][:], lhsT=qkt[:, t * P:(t + 1) * P], rhs=qkt[:, S:2 * S],
                             start=False, stop=True)

        def dve_max(i, t):
            if t == 0:
                bias = small.tile([P, NT], F32, tag="bias")
                heads[i]["bias"] = bias
            y_sb = work.tile([P, S], F32, tag="y", bufs=6)
            nc.vector.tensor_scalar(out=y_sb[:], in0=heads[i]["s%d" % t][:], scalar1=-scale, scalar2=None,
                                    op0=ALU.mult, op1=ALU.min, accum_out=heads[i]["bias"][:, t:t + 1])
            heads[i]["y%d" % t] = y_sb

        def act_exp(i, t):
            if t == 0:
                rsum = small.tile([P, NT], F32, tag="rsum")
                heads[i]["rsum"] = rsum
                e_sb = work.tile([P, NT, S], BF16, tag="e", bufs=4)
                heads[i]["e"] = e_sb
            nc.scalar.activation(out=heads[i]["e"][:, t, :], in_=heads[i]["y%d" % t][:], func=ACTF.Exp,
                                 bias=heads[i]["bias"][:, t:t + 1], scale=-1.0,
                                 accum_out=heads[i]["rsum"][:, t:t + 1])

        def pe_e_transposes(i, half):
            late = i == HEADS - 1 or (i == HEADS - 2 and half == 1)
            et_ps = psum.tile([P, 2, 2, P], F32, tag="s" if late else "et", bufs=4 if late else 2)
            for tt in range(2):
                e_words = heads[i]["e"][:, 2 * half + tt, :].bitcast(F32)
                for u in range(2):
                    nc.tensor.transpose(et_ps[:, tt, u, :], e_words[:, u * P:(u + 1) * P], ident_f[:])
            heads[i]["et%d" % half] = et_ps

        def e_copy(i, half, copy):
            if half == 0:
                eg = work.tile([P, NT * P * NT], BF16, tag="eg", bufs=3, align_bytes=64)
                heads[i]["eg"] = eg
            eg_words = heads[i]["eg"][:].bitcast(F32).rearrange("p (t q u) -> p t q u", t=NT, q=P, u=2)
            copy(out=eg_words[:, 2 * half:2 * half + 2, :, :], in_=heads[i]["et%d" % half][:].rearrange("p t u q -> p t q u"))

        def dve_quant(i, part, parts):
            if part == 0:
                e_codes = work.tile([P, S], U32, tag="ec", bufs=3, align_bytes=64)
                e_scales = work.tile([P, S], U8, tag="es", bufs=3, align_bytes=64)
                heads[i]["ec"] = e_codes
                heads[i]["es"] = e_scales
            w = S // parts
            qs = slice(part * w, (part + 1) * w)
            nc.vector.quantize_mx(out=heads[i]["ec"][:, qs].bitcast(FP8X4), scales=heads[i]["es"][:, qs],
                                  in_=heads[i]["eg"][:, part * w * NT:(part + 1) * w * NT])

        def pool_v_regroup(m, hh):
            hc = slice(hh * HD, (hh + 1) * HD)
            if hh == 0:
                vg = work.tile([P, GC, NT], BF16, tag="vg", bufs=2, align_bytes=64)
                groups[m]["vg"] = vg
            nc.gpsimd.tensor_scalar(out=groups[m]["vg"][:, hc, :].rearrange("p c (u e) -> p c u e", u=2),
                                    in0=groups[m]["v"][:, :, hc].rearrange("p (e u) c -> p c u e", e=2),
                                    scalar1=1.0, scalar2=0.0, op0=ALU.mult, op1=ALU.add)

        def dve_v_quant(m):
            v_codes = work.tile([P, GC], U32, tag="vc", bufs=3, align_bytes=64)
            v_scales = work.tile([P, GC], U8, tag="vs", bufs=3, align_bytes=64)
            nc.vector.quantize_mx(out=v_codes[:].bitcast(FP8X4), scales=v_scales[:],
                                  in_=groups[m]["vg"][:].rearrange("p c j -> p (c j)"))
            groups[m]["vc"] = v_codes
            groups[m]["vs"] = v_scales

        def pe_pv(i):
            m, b, hh = where(i)
            grp = groups[m]
            hc = slice(hh * HD, (hh + 1) * HD)
            o_ps = psum.tile([P, NT, HD], F32, tag="o", bufs=1)
            for t in range(NT):
                tq = slice(t * P, (t + 1) * P)
                nc.tensor.matmul_mx(out=o_ps[:, t, :], lhsT=heads[i]["ec"][:, tq].bitcast(FP8X4),
                                    lhsT_scale=heads[i]["es"][:, tq],
                                    rhs=grp["vc"][:, hc].bitcast(FP8X4), rhs_scale=grp["vs"][:, hc],
                                    start=True, stop=True)
            heads[i]["o"] = o_ps

        def dve_recip(i):
            recip = small.tile([P, NT], F32, tag="recip")
            nc.vector.reciprocal(out=recip[:], in_=heads[i]["rsum"][:])
            heads[i]["recip"] = recip

        def dve_out(i):
            m, b, hh = where(i)
            grp = groups[m]
            hc = slice(hh * HD, (hh + 1) * HD)
            if hh == 0:
                o_sb = work.tile([P, NT, GC], F32, tag="o_sb", bufs=2)
                grp["o"] = o_sb
            nc.vector.tensor_tensor(out=grp["o"][:, :, hc], in0=heads[i]["o"][:],
                                    in1=heads[i]["recip"][:].unsqueeze(2).to_broadcast([P, NT, HD]), op=ALU.mult)
            g = m % NG
            if m == B * NG - 1:
                nc.sync.dma_start(out=o_dram[b, :, :, g * GC + hh * HD:g * GC + (hh + 1) * HD], in_=grp["o"][:, :, hc])
            elif hh == GH - 1:
                nc.sync.dma_start(out=o_dram[b, :, :, g * GC:(g + 1) * GC], in_=grp["o"][:])

        mrow = setup_masks()
        load_group(0)
        load_group(1)
        load_group(2)
        ident_bf = const.tile([P, P], BF16)
        make_identity(nc, ident_bf[:])
        ident_f = const.tile([P, P], F32)
        make_identity(nc, ident_f[:])
        keep, maskc = setup_mask_columns(mrow)
        setup_batch(0, nc.vector)
        for hh in range(GH):
            pool_v_regroup(0, hh)
        for half in range(2):
            pe_qk_transposes(0, half)
        act_qk_copy(0)

        def live(i):
            return 0 <= i < HEADS

        for h in range(HEADS):
            for half in range(2):
                t0, t1 = 2 * half, 2 * half + 1
                if live(h - 2):
                    pe_e_transposes(h - 2, half)
                if live(h + 1) and h > 0:
                    pe_qk_transposes(h + 1, half)
                if live(h):
                    pe_deposit(h, t0)
                    pe_deposit(h, t1)
                    pe_scores(h, t0)
                if half == 0 and live(h - 3):
                    pe_pv(h - 3)
                if live(h):
                    pe_scores(h, t1)
                if h == 0:
                    pe_qk_transposes(1, half)
                if live(h - 2):
                    e_copy(h - 2, half, nc.scalar.copy)
                if half == 1 and live(h + 1):
                    act_qk_copy(h + 1)
                if half == 0:
                    if live(h - 1):
                        act_exp(h - 1, 2)
                        act_exp(h - 1, 3)
                elif live(h):
                    act_exp(h, 0)
                    act_exp(h, 1)
                if half == 1 and live(h - 2):
                    dve_quant(h - 2, 0, 1)
                if live(h):
                    dve_max(h, t0)
                    dve_max(h, t1)
                if half == 0 and live(h - 3):
                    dve_out(h - 3)
                if half == 0 and live(h - 2):
                    dve_recip(h - 2)
            if h % GH == 1 and h // GH < B * NG:
                dve_v_quant(h // GH)
            if h + GH < HEADS:
                pool_v_regroup(h // GH + 1, h % GH)
            if h % NH == 4 and h // NH + 1 < B:
                setup_batch(h // NH + 1, nc.gpsimd)
            if h % GH == 3 and h // GH + 3 < B * NG:
                load_group(h // GH + 3)

        a, b, c = HEADS - 3, HEADS - 2, HEADS - 1
        pe_e_transposes(b, 0)
        pe_e_transposes(b, 1)
        e_copy(b, 0, nc.scalar.copy)
        act_exp(c, 2)
        act_exp(c, 3)
        e_copy(b, 1, nc.vector.tensor_copy)
        dve_recip(b)
        pe_pv(a)
        dve_out(a)
        for half in range(2):
            pe_e_transposes(c, half)
            e_copy(c, half, nc.scalar.copy)
        dve_recip(c)
        dve_quant(b, 0, 1)
        dve_quant(c, 0, 2)
        pe_pv(b)
        dve_out(b)
        dve_quant(c, 1, 2)
        pe_pv(c)
        dve_out(c)
